import numpy as np
import ml_dtypes


def mxq(x, axis, fmt="e4m3"):
    dtype, down = {"e4m3": (ml_dtypes.float8_e4m3fn, 7), "e5m2": (ml_dtypes.float8_e5m2, 14)}[fmt]
    v = np.moveaxis(np.asarray(x, np.float32).astype(ml_dtypes.bfloat16).astype(np.float64), axis, -1)
    blocks = v.reshape(v.shape[:-1] + (-1, 32))
    amax = np.abs(blocks).max(-1, keepdims=True)
    byte = np.maximum(np.where(amax > 0, np.frexp(amax)[1] - 1 + 127, 0) - down, 1)
    scale = np.exp2(byte - 127.0)
    codes = (blocks / scale).astype(np.float32).astype(dtype).astype(np.float64)
    return np.moveaxis((codes * scale).reshape(v.shape), -1, axis)


WIDE = False


def mx_kscale(k):
    if not WIDE:
        return np.ones(k)
    levels = np.array([10, -10, 5, -5, 0])
    a = np.random.permutation(np.resize(levels, k // 512 * 4)).reshape(k // 512, 4)
    idx = np.arange(k)
    return np.exp2(a[idx // 512, idx % 128 // 32])


BF16 = ml_dtypes.bfloat16


def bf(x):
    return np.asarray(x, np.float32).astype(BF16)


def f64(x):
    return np.asarray(x).astype(np.float64)


B, I, H = 4096, 512, 512
GAMMA = 0.01


def sigmoid(v):
    return 1.0 / (1.0 + np.exp(-v))


def setup_inputs():
    s = mx_kscale(I)
    return {
        "x": bf(np.random.standard_normal((B, I)) * s),
        "h_prev": bf(np.random.standard_normal((B, H)) * 2.5),
        "W_r": bf(np.random.standard_normal((H, I)) * 0.7 / np.sqrt(I) / s),
        "b_r": bf(np.random.standard_normal(H) * 0.5),
        "U_r": bf(np.random.standard_normal((H, H)) * 0.28 / np.sqrt(H)),
        "V_h": bf(np.random.standard_normal((H, I)) * 0.3 / np.sqrt(I) / s),
        "b_h": bf(np.random.standard_normal(H) * 0.15),
        "W_h": bf(np.random.standard_normal((H, H)) * 0.15 / np.sqrt(H)),
    }


def reference(x, h_prev, W_r, b_r, U_r, V_h, b_h, W_h):
    h = f64(h_prev)
    xq = mxq(f64(x), 1, "e4m3")
    r = sigmoid((xq @ mxq(f64(W_r), 1, "e4m3").T) + f64(b_r) + (mxq(h, 1, "e4m3") @ mxq(f64(U_r), 1, "e4m3").T))
    A = f64(W_h) - f64(W_h).T - GAMMA * np.eye(H)
    h_reset = r * h
    return np.tanh((xq @ mxq(f64(V_h), 1, "e4m3").T) + f64(b_h) + (mxq(h_reset, 1, "e4m3") @ mxq(A, 1, "e4m3").T))

@@ -1,0 +1,286 @@
+from contextlib import ExitStack
+
+import concourse.mybir as mybir
+from concourse.masks import make_identity
+
+F32 = mybir.dt.float32
+BF16 = mybir.dt.bfloat16
+U32 = mybir.dt.uint32
+U8 = mybir.dt.uint8
+FP8X4 = mybir.dt.float8_e4m3fn_x4
+ACT = mybir.ActivationFunctionType
+ALU = mybir.AluOpType
+
+FLOPS = 4 * 2 * 4096 * 512 * 512
+
+P = 128
+ROWS = 4096
+K = 512
+CHUNK = 512
+N_CHUNKS = ROWS // CHUNK
+GAMMA = 0.01
+PINNED = False
+EXITS = (("S", "S", "V", "S"), ("S", "S", "S", "S"))
+
+
+def tile_agrucell_pa_t_kernel(tc, x, h_prev, W_r, b_r, U_r, V_h, b_h, W_h, out):
+    nc = tc.nc
+    with ExitStack() as ctx:
+        if PINNED:
+            ctx.enter_context(tc.manual_schedule())
+        keep = ctx.enter_context(tc.tile_pool(name="keep", bufs=1))
+        work = ctx.enter_context(tc.tile_pool(name="work", bufs=2))
+        psum_t = ctx.enter_context(tc.psum_pool(name="psum_t", bufs=4))
+        psum_1 = ctx.enter_context(tc.psum_pool(name="psum_1", bufs=2))
+        psum_2 = ctx.enter_context(tc.psum_pool(name="psum_2", bufs=2))
+
+        br_raw = keep.tile([P, 4], BF16, name="br_raw")
+        with nc.allow_non_contiguous_dma(reason="512 bias values, two to a piece"):
+            nc.scalar.dma_start(
+                out=br_raw[:].rearrange("p (u e) -> p u e", u=2),
+                in_=b_r.rearrange("(u p e) -> p u e", u=2, p=P, e=2),
+            )
+        bh_row = keep.tile([P, K], BF16, name="bh_row")
+        nc.vector.memset(bh_row[:], 0.0)
+        nc.scalar.dma_start(out=bh_row[0:1, :], in_=b_h.unsqueeze(0))
+
+        warm = keep.tile([P, 1], F32, name="warm")
+        nc.vector.memset(warm[:], 0.0)
+        nc.scalar.activation(out=warm[:], in_=warm[:], func=ACT.Sigmoid)
+
+        ident_f = keep.tile([P, P], F32, name="ident_f")
+        make_identity(nc, ident_f[:])
+
+        paired = "(u p e) k -> p u (e k)"
+        natural = "(j p) k -> p j k"
+
+        def load_weight(name, src, pattern):
+            raw = keep.tile([P, 4 * K], BF16, name=name)
+            if pattern == paired:
+                nc.sync.dma_start(
+                    out=raw[:].rearrange("p (u f) -> p u f", u=2),
+                    in_=src.rearrange(paired, u=2, p=P, e=2),
+                )
+            else:
+                nc.sync.dma_start(
+                    out=raw[:].rearrange("p (j k) -> p j k", j=4),
+                    in_=src.rearrange(natural, p=P),
+                )
+            return raw
+
+        x_rows = x.rearrange("(c p j) k -> c p (j k)", p=P, j=4)
+        h_rows = h_prev.rearrange("(c p j) k -> c p (j k)", p=P, j=4)
+        out_rows = out.rearrange("(c p j) n -> c p (j n)", p=P, j=4)
+        x_raw = []
+        h_raw = []
+
+        def load_chunk(c):
+            xr = keep.tile([P, 4 * K], BF16, name="x_raw%d" % c)
+            nc.sync.dma_start(out=xr[:], in_=x_rows[c])
+            x_raw.append(xr)
+            hr = keep.tile([P, 4 * K], BF16, name="h_raw%d" % c)
+            nc.sync.dma_start(out=hr[:], in_=h_rows[c])
+            h_raw.append(hr)
+
+        wr_raw = load_weight("wr_raw", W_r, paired)
+        ur_raw = load_weight("ur_raw", U_r, paired)
+        load_chunk(0)
+        vh_raw = load_weight("vh_raw", V_h, natural)
+        wn_raw = load_weight("wn_raw", W_h, natural)
+        wk_raw = load_weight("wk_raw", W_h, paired)
+        for c in range(1, N_CHUNKS):
+            load_chunk(c)
+
+        ident_b = keep.tile([P, P], BF16, name="ident_b")
+        nc.vector.tensor_copy(out=ident_b[:], in_=ident_f[:])
+        neg_ident = keep.tile([P, P], BF16, name="neg_ident")
+        nc.vector.tensor_scalar_mul(out=neg_ident[:], in0=ident_f[:], scalar1=-1.0)
+        ones = keep.tile([P, P], BF16, name="ones")
+        nc.vector.memset(ones[:], 1.0)
+        damp = keep.tile([P, 2 * 256], BF16, name="damp")
+        nc.vector.memset(damp[:], 0.0)
+        damp_v = damp[:].rearrange("p (e q f) -> p e f q", e=2, q=P, f=2)
+        for e in range(2):
+            nc.vector.tensor_scalar_mul(out=damp_v[:, e, e, :], in0=ident_f[:], scalar1=-GAMMA)
+        br = keep.tile([P, 4], F32, name="br")
+        nc.vector.tensor_copy(out=br[:], in_=br_raw[:])
+
+        def leave(engine, dst, src):
+            if engine == "S":
+                nc.scalar.copy(out=dst, in_=src)
+            else:
+                nc.vector.tensor_copy(out=dst, in_=src)
+
+        def transpose_words(raw, grouped, engines):
+            words = raw[:].bitcast(F32)
+            dst = grouped[:].bitcast(F32).rearrange("p (c u) -> p c u", u=2)
+            for half in range(2):
+                bank = psum_t.tile([P, 512], F32, name="bank_t", tag="t")
+                for u in range(2):
+                    for jj in range(2):
+                        j = 2 * half + jj
+                        nc.tensor.transpose(
+                            bank[:, (2 * u + jj) * P : (2 * u + jj + 1) * P],
+                            words[:, 256 * j + P * u : 256 * j + P * u + P],
+                            ident_f[:],
+                        )
+                leave(
+                    engines[half],
+                    dst[:, 256 * half : 256 * half + 256, :],
+                    bank[:].rearrange("p (u c) -> p c u", u=2),
+                )
+
+        def quantise(grouped, codes, scales, pieces=1):
+            w = 512 // pieces
+            for i in range(pieces):
+                nc.vector.quantize_mx(
+                    out=codes[:, i * w : (i + 1) * w].bitcast(FP8X4),
+                    scales=scales[:, i * w : (i + 1) * w],
+                    in_=grouped[:, 4 * i * w : 4 * (i + 1) * w],
+                )
+
+        def prepare_weight(name, raw):
+            grouped = keep.tile([P, 4 * K], BF16, name=name + "_g", align_bytes=64)
+            transpose_words(raw, grouped, ("V", "S"))
+            codes = keep.tile([P, K], U32, name=name + "_c", align_bytes=64)
+            scales = keep.tile([P, K], U8, name=name + "_s", align_bytes=64)
+            quantise(grouped, codes, scales)
+            return codes, scales
+
+        chunk_tiles = {}
+
+        def transposes(c):
+            xg = work.tile([P, 4 * CHUNK], BF16, name="xg", tag="xg", bufs=2, align_bytes=64)
+            hg = work.tile([P, 4 * CHUNK], BF16, name="hg", tag="hg", bufs=3, align_bytes=64)
+            xc = work.tile([P, CHUNK], U32, name="xc", tag="xc", bufs=4, align_bytes=64)
+            xs = work.tile([P, CHUNK], U8, name="xs", tag="xs", bufs=4, align_bytes=64)
+            hc = work.tile([P, CHUNK], U32, name="hc", tag="hc", bufs=3, align_bytes=64)
+            hs = work.tile([P, CHUNK], U8, name="hs", tag="hs", bufs=3, align_bytes=64)
+            engines = EXITS[c % 2]
+            transpose_words(x_raw[c], xg, engines[0:2])
+            transpose_words(h_raw[c], hg, engines[2:4])
+            quantise(xg, xc, xs)
+            quantise(hg, hc, hs)
+            chunk_tiles[c] = {"hg": hg, "xc": xc, "xs": xs, "hc": hc, "hs": hs}
+
+        def mx(acc, a, a_cols, b, b_cols, start, stop):
+            nc.tensor.matmul_mx(
+                out=acc,
+                lhsT=a[0][:, a_cols].bitcast(FP8X4),
+                lhsT_scale=a[1][:, a_cols],
+                rhs=b[0][:, b_cols].bitcast(FP8X4),
+                rhs_scale=b[1][:, b_cols],
+                start=start,
+                stop=stop,
+            )
+
+        everything = slice(0, 512)
+
+        def gate(c, t):
+            d = chunk_tiles[c]
+            if t == 0:
+                d["r"] = work.tile([P, 4 * CHUNK], F32, name="r", tag="r", bufs=2)
+            cols = slice(P * t, P * t + P)
+            acc = psum_1.tile([P, CHUNK], F32, name="acc1", tag="g")
+            mx(acc[:], wr, cols, (d["xc"], d["xs"]), everything, True, False)
+            mx(acc[:], ur, cols, (d["hc"], d["hs"]), everything, False, True)
+            nc.scalar.activation(
+                out=d["r"][:, CHUNK * t : CHUNK * (t + 1)],
+                in_=acc[:],
+                func=ACT.Sigmoid,
+                bias=br[:, t : t + 1],
+                scale=1.0,
+            )
+
+        def reset(c, pieces):
+            d = chunk_tiles[c]
+            hrg = work.tile([P, 4 * CHUNK], BF16, name="hrg", tag="hrg", bufs=2, align_bytes=64)
+            hrc = work.tile([P, CHUNK], U32, name="hrc", tag="hrc", bufs=2, align_bytes=64)
+            hrs = work.tile([P, CHUNK], U8, name="hrs", tag="hrs", bufs=2, align_bytes=64)
+            r_v = d["r"][:].rearrange("p (t b) -> p b t", t=4)
+            hg_v = d["hg"][:].rearrange("p (b t) -> p b t", t=4)
+            hrg_v = hrg[:].rearrange("p (b t) -> p b t", t=4)
+            w = CHUNK // pieces
+            for i in range(pieces):
+                rows = slice(i * w, (i + 1) * w)
+                nc.vector.tensor_tensor(
+                    out=hrg_v[:, rows, :], in0=r_v[:, rows, :], in1=hg_v[:, rows, :], op=ALU.mult
+                )
+            quantise(hrg, hrc, hrs, pieces)
+            d["hrc"] = hrc
+            d["hrs"] = hrs
+
+        def candidate(c, j, tanh_width):
+            d = chunk_tiles[c]
+            if j == 0:
+                d["z"] = work.tile([P, 4 * K], F32, name="z", tag="z", bufs=3)
+            z = d["z"]
+            cols = slice(P * j, P * j + P)
+            acc = psum_2.tile([P, K], F32, name="acc2", tag="c")
+            mx(acc[:], (d["xc"], d["xs"]), cols, vh, everything, True, False)
+            mx(acc[:], (d["hrc"], d["hrs"]), cols, am, everything, False, True)
+            nc.vector.tensor_tensor(
+                out=z[:, K * j : K * (j + 1)], in0=acc[:], in1=bias_bc[:], op=ALU.add
+            )
+            if (j + 1) % tanh_width == 0:
+                span = slice(K * (j + 1 - tanh_width), K * (j + 1))
+                nc.scalar.activation(out=z[:, span], in_=z[:, span], func=ACT.Tanh)
+                nc.sync.dma_start(out=out_rows[c][:, span], in_=z[:, span])
+
+        wr = prepare_weight("wr", wr_raw)
+        ur = prepare_weight("ur", ur_raw)
+        transposes(0)
+        vh = prepare_weight("vh", vh_raw)
+
+        a_g = keep.tile([P, 4 * K], BF16, name="a_g", align_bytes=64)
+        a_gv = a_g[:].rearrange("p (c t) -> p c t", t=4)
+        wn_v = wn_raw[:].rearrange("p (j u q e) -> p j u e q", j=4, u=2, q=P, e=2)
+        for j in range(4):
+            bank = psum_t.tile([P, 512], F32, name="bank_a", tag="t")
+            for t in range(4):
+                u, e = divmod(t, 2)
+                region = bank[:, P * t : P * t + P]
+                on_diagonal = j // 2 == u
+                nc.tensor.matmul(
+                    region,
+                    lhsT=neg_ident[:],
+                    rhs=wk_raw[:, K * t + P * j : K * t + P * j + P],
+                    start=True,
+                    stop=False,
+                )
+                nc.tensor.matmul(
+                    region, lhsT=wn_v[:, j, u, e, :], rhs=ident_b[:], start=False, stop=not on_diagonal
+                )
+                if on_diagonal:
+                    nc.tensor.matmul(
+                        region,
+                        lhsT=ident_b[:],
+                        rhs=damp[:, 256 * e + P * (j % 2) : 256 * e + P * (j % 2) + P],
+                        start=False,
+                        stop=True,
+                    )
+            leave(
+                "VS"[j % 2],
+                a_gv[:, P * j : P * j + P, :],
+                bank[:].rearrange("p (t q) -> p q t", t=4),
+            )
+        a_c = keep.tile([P, K], U32, name="a_c", align_bytes=64)
+        a_s = keep.tile([P, K], U8, name="a_s", align_bytes=64)
+        quantise(a_g, a_c, a_s)
+        am = (a_c, a_s)
+
+        bank_b = psum_t.tile([P, 512], F32, name="bank_b", tag="t")
+        nc.tensor.matmul(bank_b[:], lhsT=ones[:], rhs=bh_row[:], start=True, stop=True)
+        bias_bc = keep.tile([P, K], F32, name="bias_bc")
+        nc.vector.tensor_copy(out=bias_bc[:], in_=bank_b[:])
+
+        for c in range(N_CHUNKS):
+            if c + 1 < N_CHUNKS:
+                transposes(c + 1)
+            for i in range(4):
+                gate(c, i)
+                if c > 0:
+                    candidate(c - 1, i, 2)
+            reset(c, 2 if c + 1 < N_CHUNKS else 4)
+        for i in range(4):
+            candidate(N_CHUNKS - 1, i, 1)

@@ -19,8 +19,10 @@ K = 512
 CHUNK = 512
 N_CHUNKS = ROWS // CHUNK
 GAMMA = 0.01
-PINNED = False
-EXITS = (("S", "S", "V", "S"), ("S", "S", "S", "S"))
+PINNED = True
+WEIGHTS_ROUND = 2
+EXITS_EVEN = ("S","S","S","S")
+EXITS_ODD = ("S","S","S","S")
 
 
 def tile_agrucell_pa_t_kernel(tc, x, h_prev, W_r, b_r, U_r, V_h, b_h, W_h, out):
@@ -31,8 +33,7 @@ def tile_agrucell_pa_t_kernel(tc, x, h_prev, W_r, b_r, U_r, V_h, b_h, W_h, out):
         keep = ctx.enter_context(tc.tile_pool(name="keep", bufs=1))
         work = ctx.enter_context(tc.tile_pool(name="work", bufs=2))
         psum_t = ctx.enter_context(tc.psum_pool(name="psum_t", bufs=4))
-        psum_1 = ctx.enter_context(tc.psum_pool(name="psum_1", bufs=2))
-        psum_2 = ctx.enter_context(tc.psum_pool(name="psum_2", bufs=2))
+        psum_g = ctx.enter_context(tc.psum_pool(name="psum_g", bufs=4))
 
         br_raw = keep.tile([P, 4], BF16, name="br_raw")
         with nc.allow_non_contiguous_dma(reason="512 bias values, two to a piece"):
@@ -51,45 +52,47 @@ def tile_agrucell_pa_t_kernel(tc, x, h_prev, W_r, b_r, U_r, V_h, b_h, W_h, out):
         ident_f = keep.tile([P, P], F32, name="ident_f")
         make_identity(nc, ident_f[:])
 
-        paired = "(u p e) k -> p u (e k)"
-        natural = "(j p) k -> p j k"
-
-        def load_weight(name, src, pattern):
+        def load_weight(name, src, paired):
             raw = keep.tile([P, 4 * K], BF16, name=name)
-            if pattern == paired:
+            if paired:
                 nc.sync.dma_start(
                     out=raw[:].rearrange("p (u f) -> p u f", u=2),
-                    in_=src.rearrange(paired, u=2, p=P, e=2),
+                    in_=src.rearrange("(u p e) k -> p u (e k)", u=2, p=P, e=2),
                 )
             else:
                 nc.sync.dma_start(
                     out=raw[:].rearrange("p (j k) -> p j k", j=4),
-                    in_=src.rearrange(natural, p=P),
+                    in_=src.rearrange("(j p) k -> p j k", p=P),
                 )
             return raw
 
         x_rows = x.rearrange("(c p j) k -> c p (j k)", p=P, j=4)
         h_rows = h_prev.rearrange("(c p j) k -> c p (j k)", p=P, j=4)
         out_rows = out.rearrange("(c p j) n -> c p (j n)", p=P, j=4)
-        x_raw = []
-        h_raw = []
+        x_raw = {}
+        h_raw = {}
 
-        def load_chunk(c):
-            xr = keep.tile([P, 4 * K], BF16, name="x_raw%d" % c)
-            nc.sync.dma_start(out=xr[:], in_=x_rows[c])
-            x_raw.append(xr)
-            hr = keep.tile([P, 4 * K], BF16, name="h_raw%d" % c)
-            nc.sync.dma_start(out=hr[:], in_=h_rows[c])
-            h_raw.append(hr)
+        def load_x(c):
+            x_raw[c] = keep.tile([P, 4 * K], BF16, name="x_raw%d" % c)
+            nc.sync.dma_start(out=x_raw[c][:], in_=x_rows[c])
 
-        wr_raw = load_weight("wr_raw", W_r, paired)
-        ur_raw = load_weight("ur_raw", U_r, paired)
-        load_chunk(0)
-        vh_raw = load_weight("vh_raw", V_h, natural)
-        wn_raw = load_weight("wn_raw", W_h, natural)
-        wk_raw = load_weight("wk_raw", W_h, paired)
-        for c in range(1, N_CHUNKS):
-            load_chunk(c)
+        def load_h(c):
+            h_raw[c] = keep.tile([P, 4 * K], BF16, name="h_raw%d" % c)
+            nc.sync.dma_start(out=h_raw[c][:], in_=h_rows[c])
+
+        wr_raw = load_weight("wr_raw", W_r, True)
+        load_x(0)
+        ur_raw = load_weight("ur_raw", U_r, True)
+        load_h(0)
+        for c in (1, 2):
+            load_x(c)
+            load_h(c)
+        vh_raw = load_weight("vh_raw", V_h, False)
+        wn_raw = load_weight("wn_raw", W_h, False)
+        wk_raw = load_weight("wk_raw", W_h, True)
+        for c in range(3, N_CHUNKS):
+            load_x(c)
+            load_h(c)
 
         ident_b = keep.tile([P, P], BF16, name="ident_b")
         nc.vector.tensor_copy(out=ident_b[:], in_=ident_f[:])
@@ -111,57 +114,79 @@ def tile_agrucell_pa_t_kernel(tc, x, h_prev, W_r, b_r, U_r, V_h, b_h, W_h, out):
             else:
                 nc.vector.tensor_copy(out=dst, in_=src)
 
-        def transpose_words(raw, grouped, engines):
+        def transpose_half(raw, half):
             words = raw[:].bitcast(F32)
+            bank = psum_t.tile([P, 512], F32, name="bank_t", tag="t")
+            for u in range(2):
+                for jj in range(2):
+                    j = 2 * half + jj
+                    nc.tensor.transpose(
+                        bank[:, (2 * u + jj) * P : (2 * u + jj + 1) * P],
+                        words[:, 256 * j + P * u : 256 * j + P * u + P],
+                        ident_f[:],
+                    )
+            return bank
+
+        def leave_half(engine, bank, grouped, half):
             dst = grouped[:].bitcast(F32).rearrange("p (c u) -> p c u", u=2)
+            leave(
+                engine,
+                dst[:, 256 * half : 256 * half + 256, :],
+                bank[:].rearrange("p (u c) -> p c u", u=2),
+            )
+
+        def quantise(grouped, codes, scales, first, width):
+            nc.vector.quantize_mx(
+                out=codes[:, first : first + width].bitcast(FP8X4),
+                scales=scales[:, first : first + width],
+                in_=grouped[:, 4 * first : 4 * (first + width)],
+            )
+
+        weights = {}
+
+        def weight_transposes(raw, engines):
+            grouped = work.tile([P, 4 * K], BF16, name="w_g", tag="w_g", bufs=2, align_bytes=64)
+            banks = [transpose_half(raw, 0), transpose_half(raw, 1)]
             for half in range(2):
-                bank = psum_t.tile([P, 512], F32, name="bank_t", tag="t")
-                for u in range(2):
-                    for jj in range(2):
-                        j = 2 * half + jj
-                        nc.tensor.transpose(
-                            bank[:, (2 * u + jj) * P : (2 * u + jj + 1) * P],
-                            words[:, 256 * j + P * u : 256 * j + P * u + P],
-                            ident_f[:],
-                        )
-                leave(
-                    engines[half],
-                    dst[:, 256 * half : 256 * half + 256, :],
-                    bank[:].rearrange("p (u c) -> p c u", u=2),
-                )
+                leave_half(engines[half], banks[half], grouped, half)
+            return grouped
 
-        def quantise(grouped, codes, scales, pieces=1):
-            w = 512 // pieces
-            for i in range(pieces):
-                nc.vector.quantize_mx(
-                    out=codes[:, i * w : (i + 1) * w].bitcast(FP8X4),
-                    scales=scales[:, i * w : (i + 1) * w],
-                    in_=grouped[:, 4 * i * w : 4 * (i + 1) * w],
-                )
-
-        def prepare_weight(name, raw):
-            grouped = keep.tile([P, 4 * K], BF16, name=name + "_g", align_bytes=64)
-            transpose_words(raw, grouped, ("V", "S"))
+        def weight_quantise(name, grouped):
             codes = keep.tile([P, K], U32, name=name + "_c", align_bytes=64)
             scales = keep.tile([P, K], U8, name=name + "_s", align_bytes=64)
-            quantise(grouped, codes, scales)
-            return codes, scales
+            quantise(grouped, codes, scales, 0, K)
+            weights[name] = (codes, scales)
 
-        chunk_tiles = {}
+        tiles = {}
+        for c in range(N_CHUNKS):
+            tiles[c] = {}
 
-        def transposes(c):
-            xg = work.tile([P, 4 * CHUNK], BF16, name="xg", tag="xg", bufs=2, align_bytes=64)
-            hg = work.tile([P, 4 * CHUNK], BF16, name="hg", tag="hg", bufs=3, align_bytes=64)
-            xc = work.tile([P, CHUNK], U32, name="xc", tag="xc", bufs=4, align_bytes=64)
-            xs = work.tile([P, CHUNK], U8, name="xs", tag="xs", bufs=4, align_bytes=64)
-            hc = work.tile([P, CHUNK], U32, name="hc", tag="hc", bufs=3, align_bytes=64)
-            hs = work.tile([P, CHUNK], U8, name="hs", tag="hs", bufs=3, align_bytes=64)
-            engines = EXITS[c % 2]
-            transpose_words(x_raw[c], xg, engines[0:2])
-            transpose_words(h_raw[c], hg, engines[2:4])
-            quantise(xg, xc, xs)
-            quantise(hg, hc, hs)
-            chunk_tiles[c] = {"hg": hg, "xc": xc, "xs": xs, "hc": hc, "hs": hs}
+        def ok(c):
+            return 0 <= c < N_CHUNKS
+
+        def input_transposes(c, which, engines):
+            d = tiles[c]
+            raw = x_raw[c] if which == "x" else h_raw[c]
+            grouped = work.tile(
+                [P, 4 * CHUNK], BF16, name=which + "g", tag=which + "g", bufs=(2 if which == "x" else 3), align_bytes=64
+            )
+            d[which + "g"] = grouped
+            return [transpose_half(raw, 0), transpose_half(raw, 1)]
+
+        def input_leave(c, which, banks, engines):
+            for half in range(2):
+                leave_half(engines[half], banks[half], tiles[c][which + "g"], half)
+
+        def input_quantise(c, which):
+            d = tiles[c]
+            if which == "x":
+                codes = keep.tile([P, CHUNK], U32, name="xc%d" % c, align_bytes=64)
+                scales = keep.tile([P, CHUNK], U8, name="xs%d" % c, align_bytes=64)
+            else:
+                codes = work.tile([P, CHUNK], U32, name="hc", tag="hc", bufs=2, align_bytes=64)
+                scales = work.tile([P, CHUNK], U8, name="hs", tag="hs", bufs=2, align_bytes=64)
+            quantise(d[which + "g"], codes, scales, 0, CHUNK)
+            d[which] = (codes, scales)
 
         def mx(acc, a, a_cols, b, b_cols, start, stop):
             nc.tensor.matmul_mx(
@@ -177,13 +202,13 @@ def tile_agrucell_pa_t_kernel(tc, x, h_prev, W_r, b_r, U_r, V_h, b_h, W_h, out):
         everything = slice(0, 512)
 
         def gate(c, t):
-            d = chunk_tiles[c]
+            d = tiles[c]
             if t == 0:
                 d["r"] = work.tile([P, 4 * CHUNK], F32, name="r", tag="r", bufs=2)
             cols = slice(P * t, P * t + P)
-            acc = psum_1.tile([P, CHUNK], F32, name="acc1", tag="g")
-            mx(acc[:], wr, cols, (d["xc"], d["xs"]), everything, True, False)
-            mx(acc[:], ur, cols, (d["hc"], d["hs"]), everything, False, True)
+            acc = psum_g.tile([P, CHUNK], F32, name="acc1", tag="g")
+            mx(acc[:], weights["wr"], cols, d["x"], everything, True, False)
+            mx(acc[:], weights["ur"], cols, d["h"], everything, False, True)
             nc.scalar.activation(
                 out=d["r"][:, CHUNK * t : CHUNK * (t + 1)],
                 in_=acc[:],
@@ -192,95 +217,138 @@ def tile_agrucell_pa_t_kernel(tc, x, h_prev, W_r, b_r, U_r, V_h, b_h, W_h, out):
                 scale=1.0,
             )
 
-        def reset(c, pieces):
-            d = chunk_tiles[c]
-            hrg = work.tile([P, 4 * CHUNK], BF16, name="hrg", tag="hrg", bufs=2, align_bytes=64)
-            hrc = work.tile([P, CHUNK], U32, name="hrc", tag="hrc", bufs=2, align_bytes=64)
-            hrs = work.tile([P, CHUNK], U8, name="hrs", tag="hrs", bufs=2, align_bytes=64)
-            r_v = d["r"][:].rearrange("p (t b) -> p b t", t=4)
-            hg_v = d["hg"][:].rearrange("p (b t) -> p b t", t=4)
-            hrg_v = hrg[:].rearrange("p (b t) -> p b t", t=4)
-            w = CHUNK // pieces
-            for i in range(pieces):
-                rows = slice(i * w, (i + 1) * w)
-                nc.vector.tensor_tensor(
-                    out=hrg_v[:, rows, :], in0=r_v[:, rows, :], in1=hg_v[:, rows, :], op=ALU.mult
-                )
-            quantise(hrg, hrc, hrs, pieces)
-            d["hrc"] = hrc
-            d["hrs"] = hrs
+        def reset_product(c, first, width):
+            d = tiles[c]
+            if "hrg" not in d:
+                d["hrg"] = work.tile([P, 4 * CHUNK], BF16, name="hrg", tag="hrg", bufs=2, align_bytes=64)
+            rows = slice(first, first + width)
+            nc.vector.tensor_tensor(
+                out=d["hrg"][:].rearrange("p (b t) -> p b t", t=4)[:, rows, :],
+                in0=d["r"][:].rearrange("p (t b) -> p b t", t=4)[:, rows, :],
+                in1=d["hg"][:].rearrange("p (b t) -> p b t", t=4)[:, rows, :],
+                op=ALU.mult,
+            )
 
-        def candidate(c, j, tanh_width):
-            d = chunk_tiles[c]
+        def reset_quantise(c, first, width):
+            d = tiles[c]
+            if "hr" not in d:
+                codes = keep.tile([P, CHUNK], U32, name="hrc%d" % c, align_bytes=64)
+                scales = keep.tile([P, CHUNK], U8, name="hrs%d" % c, align_bytes=64)
+                d["hr"] = (codes, scales)
+            quantise(d["hrg"], d["hr"][0], d["hr"][1], first, width)
+
+        def candidate(c, j):
+            d = tiles[c]
             if j == 0:
                 d["z"] = work.tile([P, 4 * K], F32, name="z", tag="z", bufs=3)
-            z = d["z"]
             cols = slice(P * j, P * j + P)
-            acc = psum_2.tile([P, K], F32, name="acc2", tag="c")
-            mx(acc[:], (d["xc"], d["xs"]), cols, vh, everything, True, False)
-            mx(acc[:], (d["hrc"], d["hrs"]), cols, am, everything, False, True)
+            if j % 2 == 0:
+                acc = psum_t.tile([P, K], F32, name="acc2t", tag="t")
+            else:
+                acc = psum_g.tile([P, K], F32, name="acc2g", tag="g")
+            mx(acc[:], d["x"], cols, weights["vh"], everything, True, False)
+            mx(acc[:], d["hr"], cols, weights["a"], everything, False, True)
             nc.vector.tensor_tensor(
-                out=z[:, K * j : K * (j + 1)], in0=acc[:], in1=bias_bc[:], op=ALU.add
+                out=d["z"][:, K * j : K * (j + 1)], in0=acc[:], in1=bias_bc[:], op=ALU.add
             )
-            if (j + 1) % tanh_width == 0:
-                span = slice(K * (j + 1 - tanh_width), K * (j + 1))
-                nc.scalar.activation(out=z[:, span], in_=z[:, span], func=ACT.Tanh)
-                nc.sync.dma_start(out=out_rows[c][:, span], in_=z[:, span])
 
-        wr = prepare_weight("wr", wr_raw)
-        ur = prepare_weight("ur", ur_raw)
-        transposes(0)
-        vh = prepare_weight("vh", vh_raw)
+        def finish(c, j0, j1):
+            z = tiles[c]["z"]
+            span = slice(K * j0, K * j1)
+            nc.scalar.activation(out=z[:, span], in_=z[:, span], func=ACT.Tanh)
+            nc.sync.dma_start(out=out_rows[c][:, span], in_=z[:, span])
 
-        a_g = keep.tile([P, 4 * K], BF16, name="a_g", align_bytes=64)
-        a_gv = a_g[:].rearrange("p (c t) -> p c t", t=4)
-        wn_v = wn_raw[:].rearrange("p (j u q e) -> p j u e q", j=4, u=2, q=P, e=2)
-        for j in range(4):
-            bank = psum_t.tile([P, 512], F32, name="bank_a", tag="t")
-            for t in range(4):
-                u, e = divmod(t, 2)
-                region = bank[:, P * t : P * t + P]
-                on_diagonal = j // 2 == u
-                nc.tensor.matmul(
-                    region,
-                    lhsT=neg_ident[:],
-                    rhs=wk_raw[:, K * t + P * j : K * t + P * j + P],
-                    start=True,
-                    stop=False,
-                )
-                nc.tensor.matmul(
-                    region, lhsT=wn_v[:, j, u, e, :], rhs=ident_b[:], start=False, stop=not on_diagonal
-                )
-                if on_diagonal:
+        bias_bc = keep.tile([P, K], F32, name="bias_bc")
+
+        def second_stage_weights():
+            vh_g = weight_transposes(vh_raw, ("V", "S"))
+            a_g = work.tile([P, 4 * K], BF16, name="w_g", tag="w_g", bufs=2, align_bytes=64)
+            a_gv = a_g[:].rearrange("p (c t) -> p c t", t=4)
+            wn_v = wn_raw[:].rearrange("p (j u q e) -> p j u e q", j=4, u=2, q=P, e=2)
+            for j in range(4):
+                bank = psum_t.tile([P, 512], F32, name="bank_a", tag="t")
+                for t in range(4):
+                    u, e = divmod(t, 2)
+                    region = bank[:, P * t : P * t + P]
+                    on_diagonal = j // 2 == u
                     nc.tensor.matmul(
                         region,
-                        lhsT=ident_b[:],
-                        rhs=damp[:, 256 * e + P * (j % 2) : 256 * e + P * (j % 2) + P],
-                        start=False,
-                        stop=True,
+                        lhsT=neg_ident[:],
+                        rhs=wk_raw[:, K * t + P * j : K * t + P * j + P],
+                        start=True,
+                        stop=False,
                     )
-            leave(
-                "VS"[j % 2],
-                a_gv[:, P * j : P * j + P, :],
-                bank[:].rearrange("p (t q) -> p q t", t=4),
-            )
-        a_c = keep.tile([P, K], U32, name="a_c", align_bytes=64)
-        a_s = keep.tile([P, K], U8, name="a_s", align_bytes=64)
-        quantise(a_g, a_c, a_s)
-        am = (a_c, a_s)
+                    nc.tensor.matmul(
+                        region, lhsT=wn_v[:, j, u, e, :], rhs=ident_b[:], start=False, stop=not on_diagonal
+                    )
+                    if on_diagonal:
+                        nc.tensor.matmul(
+                            region,
+                            lhsT=ident_b[:],
+                            rhs=damp[:, 256 * e + P * (j % 2) : 256 * e + P * (j % 2) + P],
+                            start=False,
+                            stop=True,
+                        )
+                leave(
+                    "VS"[j % 2],
+                    a_gv[:, P * j : P * j + P, :],
+                    bank[:].rearrange("p (t q) -> p q t", t=4),
+                )
+            weight_quantise("vh", vh_g)
+            bank_b = psum_t.tile([P, 512], F32, name="bank_b", tag="t")
+            nc.tensor.matmul(bank_b[:], lhsT=ones[:], rhs=bh_row[:], start=True, stop=True)
+            nc.vector.tensor_copy(out=bias_bc[:], in_=bank_b[:])
+            weight_quantise("a", a_g)
 
-        bank_b = psum_t.tile([P, 512], F32, name="bank_b", tag="t")
-        nc.tensor.matmul(bank_b[:], lhsT=ones[:], rhs=bh_row[:], start=True, stop=True)
-        bias_bc = keep.tile([P, K], F32, name="bias_bc")
-        nc.vector.tensor_copy(out=bias_bc[:], in_=bank_b[:])
+        wr_g = weight_transposes(wr_raw, ("V", "S"))
+        banks = input_transposes(0, "x", None)
+        input_leave(0, "x", banks, ("V", "S"))
+        weight_quantise("wr", wr_g)
+        ur_g = weight_transposes(ur_raw, ("V", "S"))
+        input_quantise(0, "x")
+        banks = input_transposes(0, "h", None)
+        input_leave(0, "h", banks, ("V", "S"))
+        weight_quantise("ur", ur_g)
+        input_quantise(0, "h")
 
         for c in range(N_CHUNKS):
-            if c + 1 < N_CHUNKS:
-                transposes(c + 1)
-            for i in range(4):
-                gate(c, i)
-                if c > 0:
-                    candidate(c - 1, i, 2)
-            reset(c, 2 if c + 1 < N_CHUNKS else 4)
-        for i in range(4):
-            candidate(N_CHUNKS - 1, i, 1)
+            engines = EXITS_EVEN if c % 2 == 0 else EXITS_ODD
+            if ok(c + 1):
+                banks = input_transposes(c + 1, "x", None)
+            if ok(c - 1):
+                reset_product(c - 1, 0, 256)
+                reset_product(c - 1, 256, 256)
+            if ok(c + 1):
+                input_leave(c + 1, "x", banks, engines[0:2])
+            gate(c, 0)
+            gate(c, 1)
+            if ok(c - 1):
+                reset_quantise(c - 1, 0, 256)
+            if ok(c + 1):
+                input_quantise(c + 1, "x")
+                banks = input_transposes(c + 1, "h", None)
+                input_leave(c + 1, "h", banks, engines[2:4])
+            gate(c, 2)
+            gate(c, 3)
+            if ok(c - 1):
+                reset_quantise(c - 1, 256, 256)
+            if ok(c + 1):
+                input_quantise(c + 1, "h")
+            if c == WEIGHTS_ROUND:
+                second_stage_weights()
+
+        last = N_CHUNKS - 1
+        reset_product(last, 0, 128)
+        reset_product(last, 128, 128)
+        for c in range(N_CHUNKS):
+            for j in range(4):
+                candidate(c, j)
+                if c == 0:
+                    if j < 2:
+                        reset_product(last, 256 + 128 * j, 128)
+                    else:
+                        reset_quantise(last, 256 * (j - 2), 256)
+                if c == last and j >= 2:
+                    finish(c, j, j + 1)
+                elif j % 2 == 1:
+                    finish(c, j - 1, j + 1)

@@ -21,6 +21,9 @@ N_CHUNKS = ROWS // CHUNK
 GAMMA = 0.01
 PINNED = True
 WEIGHTS_ROUND = 2
+ON_GPSIMD = 0
+QUANTISE_AFTER = 20
+ONE_RUN = False
 EXITS_EVEN = ("S","S","S","S")
 EXITS_ODD = ("S","S","S","S")
 
@@ -32,6 +35,7 @@ def tile_agrucell_pa_t_kernel(tc, x, h_prev, W_r, b_r, U_r, V_h, b_h, W_h, out):
             ctx.enter_context(tc.manual_schedule())
         keep = ctx.enter_context(tc.tile_pool(name="keep", bufs=1))
         work = ctx.enter_context(tc.tile_pool(name="work", bufs=2))
+        io = ctx.enter_context(tc.tile_pool(name="io", bufs=2 * N_CHUNKS))
         psum_t = ctx.enter_context(tc.psum_pool(name="psum_t", bufs=4))
         psum_g = ctx.enter_context(tc.psum_pool(name="psum_g", bufs=4))
 
@@ -73,11 +77,11 @@ def tile_agrucell_pa_t_kernel(tc, x, h_prev, W_r, b_r, U_r, V_h, b_h, W_h, out):
         h_raw = {}
 
         def load_x(c):
-            x_raw[c] = keep.tile([P, 4 * K], BF16, name="x_raw%d" % c)
+            x_raw[c] = io.tile([P, 4 * K], BF16, name="x_raw%d" % c, tag="io")
             nc.sync.dma_start(out=x_raw[c][:], in_=x_rows[c])
 
         def load_h(c):
-            h_raw[c] = keep.tile([P, 4 * K], BF16, name="h_raw%d" % c)
+            h_raw[c] = io.tile([P, 4 * K], BF16, name="h_raw%d" % c, tag="io")
             nc.sync.dma_start(out=h_raw[c][:], in_=h_rows[c])
 
         wr_raw = load_weight("wr_raw", W_r, True)
@@ -217,12 +221,12 @@ def tile_agrucell_pa_t_kernel(tc, x, h_prev, W_r, b_r, U_r, V_h, b_h, W_h, out):
                 scale=1.0,
             )
 
-        def reset_product(c, first, width):
+        def reset_product(c, first, width, engine):
             d = tiles[c]
             if "hrg" not in d:
                 d["hrg"] = work.tile([P, 4 * CHUNK], BF16, name="hrg", tag="hrg", bufs=2, align_bytes=64)
             rows = slice(first, first + width)
-            nc.vector.tensor_tensor(
+            engine.tensor_tensor(
                 out=d["hrg"][:].rearrange("p (b t) -> p b t", t=4)[:, rows, :],
                 in0=d["r"][:].rearrange("p (t b) -> p b t", t=4)[:, rows, :],
                 in1=d["hg"][:].rearrange("p (b t) -> p b t", t=4)[:, rows, :],
@@ -239,24 +243,24 @@ def tile_agrucell_pa_t_kernel(tc, x, h_prev, W_r, b_r, U_r, V_h, b_h, W_h, out):
 
         def candidate(c, j):
             d = tiles[c]
-            if j == 0:
-                d["z"] = work.tile([P, 4 * K], F32, name="z", tag="z", bufs=3)
-            cols = slice(P * j, P * j + P)
             if j % 2 == 0:
+                d["z%d" % (j // 2)] = io.tile([P, 2 * K], F32, name="z", tag="io")
+            cols = slice(P * j, P * j + P)
+            if j % 2 == 0 or c == 0:
                 acc = psum_t.tile([P, K], F32, name="acc2t", tag="t")
             else:
                 acc = psum_g.tile([P, K], F32, name="acc2g", tag="g")
             mx(acc[:], d["x"], cols, weights["vh"], everything, True, False)
             mx(acc[:], d["hr"], cols, weights["a"], everything, False, True)
             nc.vector.tensor_tensor(
-                out=d["z"][:, K * j : K * (j + 1)], in0=acc[:], in1=bias_bc[:], op=ALU.add
+                out=d["z%d" % (j // 2)][:, K * (j % 2) : K * (j % 2 + 1)], in0=acc[:], in1=bias_bc[:], op=ALU.add
             )
 
         def finish(c, j0, j1):
-            z = tiles[c]["z"]
-            span = slice(K * j0, K * j1)
+            z = tiles[c]["z%d" % (j0 // 2)]
+            span = slice(K * (j0 % 2), K * (j0 % 2) + K * (j1 - j0))
             nc.scalar.activation(out=z[:, span], in_=z[:, span], func=ACT.Tanh)
-            nc.sync.dma_start(out=out_rows[c][:, span], in_=z[:, span])
+            nc.sync.dma_start(out=out_rows[c][:, K * j0 : K * j1], in_=z[:, span])
 
         bias_bc = keep.tile([P, K], F32, name="bias_bc")
 
@@ -311,44 +315,73 @@ def tile_agrucell_pa_t_kernel(tc, x, h_prev, W_r, b_r, U_r, V_h, b_h, W_h, out):
         weight_quantise("ur", ur_g)
         input_quantise(0, "h")
 
+        last = N_CHUNKS - 1
+        served = [0]
+
+        def next_candidate():
+            n = served[0]
+            c, j = divmod(n, 4)
+            candidate(c, j)
+            if c == last and j >= 2:
+                finish(c, j, j + 1)
+            elif j % 2 == 1:
+                finish(c, j - 1, j + 1)
+            served[0] = n + 1
+
+        def product_on_gpsimd(c):
+            for j in range(4):
+                reset_product(c, P * j, P, nc.gpsimd)
+
         for c in range(N_CHUNKS):
             engines = EXITS_EVEN if c % 2 == 0 else EXITS_ODD
+            weave = ON_GPSIMD > 0 and c == last
+            vector_multiplies = ok(c - 1) and c - 1 < N_CHUNKS - ON_GPSIMD
             if ok(c + 1):
                 banks = input_transposes(c + 1, "x", None)
-            if ok(c - 1):
-                reset_product(c - 1, 0, 256)
-                reset_product(c - 1, 256, 256)
+                if ONE_RUN:
+                    banks_h = input_transposes(c + 1, "h", None)
+            if vector_multiplies:
+                reset_product(c - 1, 0, 256, nc.vector)
+                reset_product(c - 1, 256, 256, nc.vector)
+            elif ok(c - 1):
+                product_on_gpsimd(c - 1)
             if ok(c + 1):
                 input_leave(c + 1, "x", banks, engines[0:2])
-            gate(c, 0)
-            gate(c, 1)
-            if ok(c - 1):
+            for t in (0, 1):
+                gate(c, t)
+                if weave:
+                    next_candidate()
+            if vector_multiplies:
                 reset_quantise(c - 1, 0, 256)
             if ok(c + 1):
                 input_quantise(c + 1, "x")
-                banks = input_transposes(c + 1, "h", None)
-                input_leave(c + 1, "h", banks, engines[2:4])
-            gate(c, 2)
-            gate(c, 3)
-            if ok(c - 1):
+                if not ONE_RUN:
+                    banks_h = input_transposes(c + 1, "h", None)
+                input_leave(c + 1, "h", banks_h, engines[2:4])
+            for t in (2, 3):
+                gate(c, t)
+                if weave:
+                    next_candidate()
+            if vector_multiplies:
                 reset_quantise(c - 1, 256, 256)
             if ok(c + 1):
                 input_quantise(c + 1, "h")
             if c == WEIGHTS_ROUND:
                 second_stage_weights()
 
-        last = N_CHUNKS - 1
-        reset_product(last, 0, 128)
-        reset_product(last, 128, 128)
-        for c in range(N_CHUNKS):
-            for j in range(4):
-                candidate(c, j)
-                if c == 0:
-                    if j < 2:
-                        reset_product(last, 256 + 128 * j, 128)
-                    else:
-                        reset_quantise(last, 256 * (j - 2), 256)
-                if c == last and j >= 2:
-                    finish(c, j, j + 1)
-                elif j % 2 == 1:
-                    finish(c, j - 1, j + 1)
+        if ON_GPSIMD > 0:
+            product_on_gpsimd(last)
+        else:
+            reset_product(last, 0, 128, nc.vector)
+            reset_product(last, 128, 128, nc.vector)
+        while served[0] < 4 * N_CHUNKS:
+            next_candidate()
+            n = served[0]
+            if ON_GPSIMD == 0:
+                if n <= 2:
+                    reset_product(last, 128 + 128 * n, 128, nc.vector)
+                elif n <= 4:
+                    reset_quantise(last, 256 * (n - 3), 256)
+            elif n == QUANTISE_AFTER:
+                for c in range(N_CHUNKS - ON_GPSIMD, N_CHUNKS):
+                    reset_quantise(c, 0, CHUNK)

@@ -21,7 +21,7 @@ N_CHUNKS = ROWS // CHUNK
 GAMMA = 0.01
 PINNED = True
 WEIGHTS_ROUND = 2
-ON_GPSIMD = 0
+ON_GPSIMD = 2
 QUANTISE_AFTER = 20
 ONE_RUN = False
 EXITS_EVEN = ("S","S","S","S")

@@ -25,7 +25,7 @@ ON_GPSIMD = 2
 QUANTISE_AFTER = 20
 ONE_RUN = False
 EXITS_EVEN = ("S","S","S","S")
-EXITS_ODD = ("S","S","S","S")
+EXITS_ODD = ("S","S","V","S")
 
 
 def tile_agrucell_pa_t_kernel(tc, x, h_prev, W_r, b_r, U_r, V_h, b_h, W_h, out):

@@ -25,7 +25,7 @@ ON_GPSIMD = 2
 QUANTISE_AFTER = 20
 ONE_RUN = False
 EXITS_EVEN = ("S","S","S","S")
-EXITS_ODD = ("S","S","V","S")
+EXITS_ODD = ("S","S","S","S")
 
 
 def tile_agrucell_pa_t_kernel(tc, x, h_prev, W_r, b_r, U_r, V_h, b_h, W_h, out):
@@ -221,17 +221,26 @@ def tile_agrucell_pa_t_kernel(tc, x, h_prev, W_r, b_r, U_r, V_h, b_h, W_h, out):
                 scale=1.0,
             )
 
-        def reset_product(c, first, width, engine):
+        def reset_product(c, first, width, on_vector):
             d = tiles[c]
             if "hrg" not in d:
                 d["hrg"] = work.tile([P, 4 * CHUNK], BF16, name="hrg", tag="hrg", bufs=2, align_bytes=64)
-            rows = slice(first, first + width)
-            engine.tensor_tensor(
-                out=d["hrg"][:].rearrange("p (b t) -> p b t", t=4)[:, rows, :],
-                in0=d["r"][:].rearrange("p (t b) -> p b t", t=4)[:, rows, :],
-                in1=d["hg"][:].rearrange("p (b t) -> p b t", t=4)[:, rows, :],
-                op=ALU.mult,
-            )
+            if on_vector:
+                runs = slice(first // 4, (first + width) // 4)
+                nc.vector.tensor_tensor(
+                    out=d["hrg"][:].rearrange("p (c i t) -> p c t i", i=4, t=4)[:, runs, :, :],
+                    in0=d["r"][:].rearrange("p (t c i) -> p c t i", t=4, i=4)[:, runs, :, :],
+                    in1=d["hg"][:].rearrange("p (c i t) -> p c t i", i=4, t=4)[:, runs, :, :],
+                    op=ALU.mult,
+                )
+            else:
+                rows = slice(first, first + width)
+                nc.gpsimd.tensor_tensor(
+                    out=d["hrg"][:].rearrange("p (b t) -> p b t", t=4)[:, rows, :],
+                    in0=d["r"][:].rearrange("p (t b) -> p b t", t=4)[:, rows, :],
+                    in1=d["hg"][:].rearrange("p (b t) -> p b t", t=4)[:, rows, :],
+                    op=ALU.mult,
+                )
 
         def reset_quantise(c, first, width):
             d = tiles[c]
@@ -330,7 +339,7 @@ def tile_agrucell_pa_t_kernel(tc, x, h_prev, W_r, b_r, U_r, V_h, b_h, W_h, out):
 
         def product_on_gpsimd(c):
             for j in range(4):
-                reset_product(c, P * j, P, nc.gpsimd)
+                reset_product(c, P * j, P, False)
 
         for c in range(N_CHUNKS):
             engines = EXITS_EVEN if c % 2 == 0 else EXITS_ODD
@@ -341,8 +350,7 @@ def tile_agrucell_pa_t_kernel(tc, x, h_prev, W_r, b_r, U_r, V_h, b_h, W_h, out):
                 if ONE_RUN:
                     banks_h = input_transposes(c + 1, "h", None)
             if vector_multiplies:
-                reset_product(c - 1, 0, 256, nc.vector)
-                reset_product(c - 1, 256, 256, nc.vector)
+                reset_product(c - 1, 0, CHUNK, True)
             elif ok(c - 1):
                 product_on_gpsimd(c - 1)
             if ok(c + 1):
@@ -351,8 +359,6 @@ def tile_agrucell_pa_t_kernel(tc, x, h_prev, W_r, b_r, U_r, V_h, b_h, W_h, out):
                 gate(c, t)
                 if weave:
                     next_candidate()
-            if vector_multiplies:
-                reset_quantise(c - 1, 0, 256)
             if ok(c + 1):
                 input_quantise(c + 1, "x")
                 if not ONE_RUN:
@@ -363,7 +369,7 @@ def tile_agrucell_pa_t_kernel(tc, x, h_prev, W_r, b_r, U_r, V_h, b_h, W_h, out):
                 if weave:
                     next_candidate()
             if vector_multiplies:
-                reset_quantise(c - 1, 256, 256)
+                reset_quantise(c - 1, 0, CHUNK)
             if ok(c + 1):
                 input_quantise(c + 1, "h")
             if c == WEIGHTS_ROUND:
@@ -372,14 +378,14 @@ def tile_agrucell_pa_t_kernel(tc, x, h_prev, W_r, b_r, U_r, V_h, b_h, W_h, out):
         if ON_GPSIMD > 0:
             product_on_gpsimd(last)
         else:
-            reset_product(last, 0, 128, nc.vector)
-            reset_product(last, 128, 128, nc.vector)
+            reset_product(last, 0, 128, True)
+            reset_product(last, 128, 128, True)
         while served[0] < 4 * N_CHUNKS:
             next_candidate()
             n = served[0]
             if ON_GPSIMD == 0:
                 if n <= 2:
-                    reset_product(last, 128 + 128 * n, 128, nc.vector)
+                    reset_product(last, 128 + 128 * n, 128, True)
                 elif n <= 4:
                     reset_quantise(last, 256 * (n - 3), 256)
             elif n == QUANTISE_AFTER:

@@ -23,7 +23,6 @@ PINNED = True
 WEIGHTS_ROUND = 2
 ON_GPSIMD = 2
 QUANTISE_AFTER = 20
-ONE_RUN = False
 EXITS_EVEN = ("S","S","S","S")
 EXITS_ODD = ("S","S","S","S")
 
@@ -347,31 +346,22 @@ def tile_agrucell_pa_t_kernel(tc, x, h_prev, W_r, b_r, U_r, V_h, b_h, W_h, out):
             vector_multiplies = ok(c - 1) and c - 1 < N_CHUNKS - ON_GPSIMD
             if ok(c + 1):
                 banks = input_transposes(c + 1, "x", None)
-                if ONE_RUN:
-                    banks_h = input_transposes(c + 1, "h", None)
+                banks_h = input_transposes(c + 1, "h", None)
             if vector_multiplies:
                 reset_product(c - 1, 0, CHUNK, True)
             elif ok(c - 1):
                 product_on_gpsimd(c - 1)
             if ok(c + 1):
                 input_leave(c + 1, "x", banks, engines[0:2])
-            for t in (0, 1):
-                gate(c, t)
-                if weave:
-                    next_candidate()
-            if ok(c + 1):
-                input_quantise(c + 1, "x")
-                if not ONE_RUN:
-                    banks_h = input_transposes(c + 1, "h", None)
                 input_leave(c + 1, "h", banks_h, engines[2:4])
-            for t in (2, 3):
+                input_quantise(c + 1, "x")
+                input_quantise(c + 1, "h")
+            for t in range(4):
                 gate(c, t)
                 if weave:
                     next_candidate()
             if vector_multiplies:
                 reset_quantise(c - 1, 0, CHUNK)
-            if ok(c + 1):
-                input_quantise(c + 1, "h")
             if c == WEIGHTS_ROUND:
                 second_stage_weights()
 

@@ -225,11 +225,11 @@ def tile_agrucell_pa_t_kernel(tc, x, h_prev, W_r, b_r, U_r, V_h, b_h, W_h, out):
             if "hrg" not in d:
                 d["hrg"] = work.tile([P, 4 * CHUNK], BF16, name="hrg", tag="hrg", bufs=2, align_bytes=64)
             if on_vector:
-                runs = slice(first // 4, (first + width) // 4)
+                runs = slice(first // 2, (first + width) // 2)
                 nc.vector.tensor_tensor(
-                    out=d["hrg"][:].rearrange("p (c i t) -> p c t i", i=4, t=4)[:, runs, :, :],
-                    in0=d["r"][:].rearrange("p (t c i) -> p c t i", t=4, i=4)[:, runs, :, :],
-                    in1=d["hg"][:].rearrange("p (c i t) -> p c t i", i=4, t=4)[:, runs, :, :],
+                    out=d["hrg"][:].rearrange("p (c i t) -> p c t i", i=2, t=4)[:, runs, :, :],
+                    in0=d["r"][:].rearrange("p (t c i) -> p c t i", t=4, i=2)[:, runs, :, :],
+                    in1=d["hg"][:].rearrange("p (c i t) -> p c t i", i=2, t=4)[:, runs, :, :],
                     op=ALU.mult,
                 )
             else:

@@ -22,7 +22,6 @@ GAMMA = 0.01
 PINNED = True
 WEIGHTS_ROUND = 2
 ON_GPSIMD = 2
-QUANTISE_AFTER = 20
 EXITS_EVEN = ("S","S","S","S")
 EXITS_ODD = ("S","S","S","S")
 
@@ -378,6 +377,5 @@ def tile_agrucell_pa_t_kernel(tc, x, h_prev, W_r, b_r, U_r, V_h, b_h, W_h, out):
                     reset_product(last, 128 + 128 * n, 128, True)
                 elif n <= 4:
                     reset_quantise(last, 256 * (n - 3), 256)
-            elif n == QUANTISE_AFTER:
-                for c in range(N_CHUNKS - ON_GPSIMD, N_CHUNKS):
-                    reset_quantise(c, 0, CHUNK)
+            elif n % 4 == 2 and n // 4 + 1 >= N_CHUNKS - ON_GPSIMD and n // 4 + 1 < N_CHUNKS:
+                reset_quantise(n // 4 + 1, 0, CHUNK)

@@ -19,18 +19,14 @@ K = 512
 CHUNK = 512
 N_CHUNKS = ROWS // CHUNK
 GAMMA = 0.01
-PINNED = True
-WEIGHTS_ROUND = 2
-ON_GPSIMD = 2
-EXITS_EVEN = ("S","S","S","S")
-EXITS_ODD = ("S","S","S","S")
+FIRST_WOVEN = 5
+V_ROWS = [512, 512, 512, 512, 256, 256, 256, 0]
 
 
 def tile_agrucell_pa_t_kernel(tc, x, h_prev, W_r, b_r, U_r, V_h, b_h, W_h, out):
     nc = tc.nc
     with ExitStack() as ctx:
-        if PINNED:
-            ctx.enter_context(tc.manual_schedule())
+        ctx.enter_context(tc.manual_schedule())
         keep = ctx.enter_context(tc.tile_pool(name="keep", bufs=1))
         work = ctx.enter_context(tc.tile_pool(name="work", bufs=2))
         io = ctx.enter_context(tc.tile_pool(name="io", bufs=2 * N_CHUNKS))
@@ -159,6 +155,7 @@ def tile_agrucell_pa_t_kernel(tc, x, h_prev, W_r, b_r, U_r, V_h, b_h, W_h, out):
             quantise(grouped, codes, scales, 0, K)
             weights[name] = (codes, scales)
 
+        last = N_CHUNKS - 1
         tiles = {}
         for c in range(N_CHUNKS):
             tiles[c] = {}
@@ -206,7 +203,7 @@ def tile_agrucell_pa_t_kernel(tc, x, h_prev, W_r, b_r, U_r, V_h, b_h, W_h, out):
         def gate(c, t):
             d = tiles[c]
             if t == 0:
-                d["r"] = work.tile([P, 4 * CHUNK], F32, name="r", tag="r", bufs=2)
+                d["r"] = work.tile([P, 4 * CHUNK], F32, name="r", tag="r", bufs=3)
             cols = slice(P * t, P * t + P)
             acc = psum_g.tile([P, CHUNK], F32, name="acc1", tag="g")
             mx(acc[:], weights["wr"], cols, d["x"], everything, True, False)
@@ -222,7 +219,7 @@ def tile_agrucell_pa_t_kernel(tc, x, h_prev, W_r, b_r, U_r, V_h, b_h, W_h, out):
         def reset_product(c, first, width, on_vector):
             d = tiles[c]
             if "hrg" not in d:
-                d["hrg"] = work.tile([P, 4 * CHUNK], BF16, name="hrg", tag="hrg", bufs=2, align_bytes=64)
+                d["hrg"] = work.tile([P, 4 * CHUNK], BF16, name="hrg", tag="hrg", bufs=3, align_bytes=64)
             if on_vector:
                 runs = slice(first // 2, (first + width) // 2)
                 nc.vector.tensor_tensor(
@@ -248,19 +245,26 @@ def tile_agrucell_pa_t_kernel(tc, x, h_prev, W_r, b_r, U_r, V_h, b_h, W_h, out):
                 d["hr"] = (codes, scales)
             quantise(d["hrg"], d["hr"][0], d["hr"][1], first, width)
 
-        def candidate(c, j):
+        def candidate_multiply(c, j, pool):
             d = tiles[c]
-            if j % 2 == 0:
-                d["z%d" % (j // 2)] = io.tile([P, 2 * K], F32, name="z", tag="io")
             cols = slice(P * j, P * j + P)
-            if j % 2 == 0 or c == 0:
+            if pool is psum_t:
                 acc = psum_t.tile([P, K], F32, name="acc2t", tag="t")
             else:
                 acc = psum_g.tile([P, K], F32, name="acc2g", tag="g")
             mx(acc[:], d["x"], cols, weights["vh"], everything, True, False)
             mx(acc[:], d["hr"], cols, weights["a"], everything, False, True)
+            d["acc%d" % j] = acc
+
+        def candidate_add(c, j):
+            d = tiles[c]
+            if j % 2 == 0:
+                d["z%d" % (j // 2)] = io.tile([P, 2 * K], F32, name="z", tag="io")
             nc.vector.tensor_tensor(
-                out=d["z%d" % (j // 2)][:, K * (j % 2) : K * (j % 2 + 1)], in0=acc[:], in1=bias_bc[:], op=ALU.add
+                out=d["z%d" % (j // 2)][:, K * (j % 2) : K * (j % 2 + 1)],
+                in0=d["acc%d" % j][:],
+                in1=bias_bc[:],
+                op=ALU.add,
             )
 
         def finish(c, j0, j1):
@@ -271,45 +275,60 @@ def tile_agrucell_pa_t_kernel(tc, x, h_prev, W_r, b_r, U_r, V_h, b_h, W_h, out):
 
         bias_bc = keep.tile([P, K], F32, name="bias_bc")
 
-        def second_stage_weights():
-            vh_g = weight_transposes(vh_raw, ("V", "S"))
-            a_g = work.tile([P, 4 * K], BF16, name="w_g", tag="w_g", bufs=2, align_bytes=64)
+        vh_g = work.tile([P, 4 * K], BF16, name="vh_g", tag="vh_g", bufs=1, align_bytes=64)
+        a_g = work.tile([P, 4 * K], BF16, name="a_g", tag="a_g", bufs=1, align_bytes=64)
+
+        def vh_half(half, engine):
+            leave_half(engine, transpose_half(vh_raw, half), vh_g, half)
+
+        def a_block(j, engine):
             a_gv = a_g[:].rearrange("p (c t) -> p c t", t=4)
             wn_v = wn_raw[:].rearrange("p (j u q e) -> p j u e q", j=4, u=2, q=P, e=2)
-            for j in range(4):
-                bank = psum_t.tile([P, 512], F32, name="bank_a", tag="t")
-                for t in range(4):
-                    u, e = divmod(t, 2)
-                    region = bank[:, P * t : P * t + P]
-                    on_diagonal = j // 2 == u
+            bank = psum_t.tile([P, 512], F32, name="bank_a", tag="t")
+            for t in range(4):
+                u, e = divmod(t, 2)
+                region = bank[:, P * t : P * t + P]
+                on_diagonal = j // 2 == u
+                nc.tensor.matmul(
+                    region,
+                    lhsT=neg_ident[:],
+                    rhs=wk_raw[:, K * t + P * j : K * t + P * j + P],
+                    start=True,
+                    stop=False,
+                )
+                nc.tensor.matmul(region, lhsT=wn_v[:, j, u, e, :], rhs=ident_b[:], start=False, stop=not on_diagonal)
+                if on_diagonal:
                     nc.tensor.matmul(
                         region,
-                        lhsT=neg_ident[:],
-                        rhs=wk_raw[:, K * t + P * j : K * t + P * j + P],
-                        start=True,
-                        stop=False,
+                        lhsT=ident_b[:],
+                        rhs=damp[:, 256 * e + P * (j % 2) : 256 * e + P * (j % 2) + P],
+                        start=False,
+                        stop=True,
                     )
-                    nc.tensor.matmul(
-                        region, lhsT=wn_v[:, j, u, e, :], rhs=ident_b[:], start=False, stop=not on_diagonal
-                    )
-                    if on_diagonal:
-                        nc.tensor.matmul(
-                            region,
-                            lhsT=ident_b[:],
-                            rhs=damp[:, 256 * e + P * (j % 2) : 256 * e + P * (j % 2) + P],
-                            start=False,
-                            stop=True,
-                        )
-                leave(
-                    "VS"[j % 2],
-                    a_gv[:, P * j : P * j + P, :],
-                    bank[:].rearrange("p (t q) -> p q t", t=4),
-                )
-            weight_quantise("vh", vh_g)
+            leave(engine, a_gv[:, P * j : P * j + P, :], bank[:].rearrange("p (t q) -> p q t", t=4))
+
+        def bias_block():
             bank_b = psum_t.tile([P, 512], F32, name="bank_b", tag="t")
             nc.tensor.matmul(bank_b[:], lhsT=ones[:], rhs=bh_row[:], start=True, stop=True)
             nc.vector.tensor_copy(out=bias_bc[:], in_=bank_b[:])
-            weight_quantise("a", a_g)
+
+        def weights_in_round(c):
+            if c == 1:
+                vh_half(1, "V")
+            elif c == 2:
+                a_block(0, "S")
+                a_block(1, "S")
+            elif c == 3:
+                a_block(2, "V")
+                a_block(3, "S")
+            elif c == 4:
+                bias_block()
+                weight_quantise("a", a_g)
+
+        def weights_after_round(c):
+            if c == 1:
+                vh_half(0, "S")
+                weight_quantise("vh", vh_g)
 
         wr_g = weight_transposes(wr_raw, ("V", "S"))
         banks = input_transposes(0, "x", None)
@@ -322,60 +341,82 @@ def tile_agrucell_pa_t_kernel(tc, x, h_prev, W_r, b_r, U_r, V_h, b_h, W_h, out):
         weight_quantise("ur", ur_g)
         input_quantise(0, "h")
 
-        last = N_CHUNKS - 1
         served = [0]
+        waiting = []
 
-        def next_candidate():
+        def multiply_pair(pools):
             n = served[0]
             c, j = divmod(n, 4)
-            candidate(c, j)
-            if c == last and j >= 2:
-                finish(c, j, j + 1)
-            elif j % 2 == 1:
-                finish(c, j - 1, j + 1)
-            served[0] = n + 1
+            for i in range(2):
+                candidate_multiply(c, j + i, pools[i])
+            served[0] = n + 2
+            waiting.append((c, j))
+
+        def add_pair():
+            c, j = waiting[0]
+            candidate_add(c, j)
+            candidate_add(c, j + 1)
+
+        def finish_pair():
+            c, j = waiting.pop(0)
+            finish(c, j, j + 2)
 
         def product_on_gpsimd(c):
-            for j in range(4):
-                reset_product(c, P * j, P, False)
+            for first in range(V_ROWS[c], CHUNK, P):
+                reset_product(c, first, P, False)
 
         for c in range(N_CHUNKS):
-            engines = EXITS_EVEN if c % 2 == 0 else EXITS_ODD
-            weave = ON_GPSIMD > 0 and c == last
-            vector_multiplies = ok(c - 1) and c - 1 < N_CHUNKS - ON_GPSIMD
+            woven = c >= FIRST_WOVEN
             if ok(c + 1):
-                banks = input_transposes(c + 1, "x", None)
+                banks_x = input_transposes(c + 1, "x", None)
                 banks_h = input_transposes(c + 1, "h", None)
-            if vector_multiplies:
-                reset_product(c - 1, 0, CHUNK, True)
-            elif ok(c - 1):
-                product_on_gpsimd(c - 1)
+            if ok(c - 2) and V_ROWS[c - 2] < CHUNK:
+                reset_quantise(c - 2, 0, CHUNK)
             if ok(c + 1):
-                input_leave(c + 1, "x", banks, engines[0:2])
-                input_leave(c + 1, "h", banks_h, engines[2:4])
+                input_leave(c + 1, "x", banks_x, "SV" if c < 3 else "SS")
+            if woven:
+                multiply_pair((psum_g, psum_g))
+            if ok(c + 1):
+                input_leave(c + 1, "h", banks_h, "SS")
+            gate(c, 0)
+            if woven:
+                add_pair()
+            gate(c, 1)
+            if woven:
+                multiply_pair((psum_g, psum_g))
+                finish_pair()
+            if ok(c - 1) and V_ROWS[c - 1] > 0:
+                reset_product(c - 1, 0, V_ROWS[c - 1], True)
+            gate(c, 2)
+            if ok(c + 1):
                 input_quantise(c + 1, "x")
+            gate(c, 3)
+            weights_in_round(c)
+            if woven:
+                add_pair()
+            if ok(c + 1):
                 input_quantise(c + 1, "h")
-            for t in range(4):
-                gate(c, t)
-                if weave:
-                    next_candidate()
-            if vector_multiplies:
+            if ok(c - 1):
+                product_on_gpsimd(c - 1)
+            if woven:
+                finish_pair()
+            weights_after_round(c)
+            if ok(c - 1) and V_ROWS[c - 1] == CHUNK:
                 reset_quantise(c - 1, 0, CHUNK)
-            if c == WEIGHTS_ROUND:
-                second_stage_weights()
 
-        if ON_GPSIMD > 0:
-            product_on_gpsimd(last)
-        else:
-            reset_product(last, 0, 128, True)
-            reset_product(last, 128, 128, True)
+        product_on_gpsimd(last)
+        reset_quantise(last - 1, 0, CHUNK)
         while served[0] < 4 * N_CHUNKS:
-            next_candidate()
             n = served[0]
-            if ON_GPSIMD == 0:
-                if n <= 2:
-                    reset_product(last, 128 + 128 * n, 128, True)
-                elif n <= 4:
-                    reset_quantise(last, 256 * (n - 3), 256)
-            elif n % 4 == 2 and n // 4 + 1 >= N_CHUNKS - ON_GPSIMD and n // 4 + 1 < N_CHUNKS:
-                reset_quantise(n // 4 + 1, 0, CHUNK)
+            c, j = divmod(n, 4)
+            for i in range(2):
+                candidate_multiply(c, j + i, (psum_g, psum_t)[i])
+                candidate_add(c, j + i)
+            served[0] = n + 2
+            if c == last and j == 2:
+                finish(c, 2, 3)
+                finish(c, 3, 4)
+            else:
+                finish(c, j, j + 2)
+            if served[0] == 24:
+                reset_quantise(last, 0, CHUNK)

@@ -19,8 +19,8 @@ K = 512
 CHUNK = 512
 N_CHUNKS = ROWS // CHUNK
 GAMMA = 0.01
-FIRST_WOVEN = 5
-V_ROWS = [512, 512, 512, 512, 256, 256, 256, 0]
+WOVEN = [0, 0, 0, 0, 0, 6, 6, 4]
+V_ROWS = [512, 512, 512, 384, 128, 128, 384, 0]
 
 
 def tile_agrucell_pa_t_kernel(tc, x, h_prev, W_r, b_r, U_r, V_h, b_h, W_h, out):
@@ -312,23 +312,20 @@ def tile_agrucell_pa_t_kernel(tc, x, h_prev, W_r, b_r, U_r, V_h, b_h, W_h, out):
             nc.tensor.matmul(bank_b[:], lhsT=ones[:], rhs=bh_row[:], start=True, stop=True)
             nc.vector.tensor_copy(out=bias_bc[:], in_=bank_b[:])
 
-        def weights_in_round(c):
-            if c == 1:
-                vh_half(1, "V")
-            elif c == 2:
-                a_block(0, "S")
-                a_block(1, "S")
-            elif c == 3:
-                a_block(2, "V")
-                a_block(3, "S")
-            elif c == 4:
-                bias_block()
-                weight_quantise("a", a_g)
-
         def weights_after_round(c):
             if c == 1:
-                vh_half(0, "S")
+                vh_half(1, "S")
+                vh_half(0, "V")
                 weight_quantise("vh", vh_g)
+                a_block(0, "S")
+            elif c == 2:
+                a_block(1, "S")
+            elif c == 3:
+                a_block(2, "S")
+                a_block(3, "S")
+                bias_block()
+            elif c == 4:
+                weight_quantise("a", a_g)
 
         wr_g = weight_transposes(wr_raw, ("V", "S"))
         banks = input_transposes(0, "x", None)
@@ -342,81 +339,75 @@ def tile_agrucell_pa_t_kernel(tc, x, h_prev, W_r, b_r, U_r, V_h, b_h, W_h, out):
         input_quantise(0, "h")
 
         served = [0]
-        waiting = []
+        summed = []
+        added = []
 
-        def multiply_pair(pools):
-            n = served[0]
-            c, j = divmod(n, 4)
-            for i in range(2):
-                candidate_multiply(c, j + i, pools[i])
-            served[0] = n + 2
-            waiting.append((c, j))
+        def multiply_tiles(count):
+            for i in range(count):
+                c, j = divmod(served[0], 4)
+                candidate_multiply(c, j, psum_g)
+                summed.append((c, j))
+                served[0] += 1
 
-        def add_pair():
-            c, j = waiting[0]
-            candidate_add(c, j)
-            candidate_add(c, j + 1)
+        def add_tiles():
+            for c, j in summed:
+                candidate_add(c, j)
+            added.extend(summed)
+            summed.clear()
 
-        def finish_pair():
-            c, j = waiting.pop(0)
-            finish(c, j, j + 2)
+        def finish_tiles():
+            while added and (len(added) > 1 or added[0] >= (last, 2)):
+                c, j = added.pop(0)
+                if (c, j) >= (last, 2):
+                    finish(c, j, j + 1)
+                else:
+                    added.pop(0)
+                    finish(c, j, j + 2)
 
         def product_on_gpsimd(c):
             for first in range(V_ROWS[c], CHUNK, P):
                 reset_product(c, first, P, False)
 
         for c in range(N_CHUNKS):
-            woven = c >= FIRST_WOVEN
-            if ok(c + 1):
-                banks_x = input_transposes(c + 1, "x", None)
-                banks_h = input_transposes(c + 1, "h", None)
+            if ok(c - 1):
+                product_on_gpsimd(c - 1)
             if ok(c - 2) and V_ROWS[c - 2] < CHUNK:
                 reset_quantise(c - 2, 0, CHUNK)
             if ok(c + 1):
-                input_leave(c + 1, "x", banks_x, "SV" if c < 3 else "SS")
-            if woven:
-                multiply_pair((psum_g, psum_g))
+                banks_x = input_transposes(c + 1, "x", None)
+                banks_h = input_transposes(c + 1, "h", None)
+            multiply_tiles(WOVEN[c] // 2)
+            if ok(c + 1):
+                input_leave(c + 1, "x", banks_x, "VS")
+            add_tiles()
             if ok(c + 1):
                 input_leave(c + 1, "h", banks_h, "SS")
             gate(c, 0)
-            if woven:
-                add_pair()
-            gate(c, 1)
-            if woven:
-                multiply_pair((psum_g, psum_g))
-                finish_pair()
+            finish_tiles()
+            multiply_tiles(WOVEN[c] // 2)
+            add_tiles()
             if ok(c - 1) and V_ROWS[c - 1] > 0:
                 reset_product(c - 1, 0, V_ROWS[c - 1], True)
-            gate(c, 2)
             if ok(c + 1):
                 input_quantise(c + 1, "x")
-            gate(c, 3)
-            weights_in_round(c)
-            if woven:
-                add_pair()
+            for t in (1, 2, 3):
+                gate(c, t)
+            finish_tiles()
             if ok(c + 1):
                 input_quantise(c + 1, "h")
-            if ok(c - 1):
-                product_on_gpsimd(c - 1)
-            if woven:
-                finish_pair()
-            weights_after_round(c)
             if ok(c - 1) and V_ROWS[c - 1] == CHUNK:
                 reset_quantise(c - 1, 0, CHUNK)
+            weights_after_round(c)
 
         product_on_gpsimd(last)
         reset_quantise(last - 1, 0, CHUNK)
         while served[0] < 4 * N_CHUNKS:
-            n = served[0]
-            c, j = divmod(n, 4)
-            for i in range(2):
-                candidate_multiply(c, j + i, (psum_g, psum_t)[i])
-                candidate_add(c, j + i)
-            served[0] = n + 2
-            if c == last and j == 2:
-                finish(c, 2, 3)
-                finish(c, 3, 4)
-            else:
-                finish(c, j, j + 2)
-            if served[0] == 24:
+            for pool in (psum_g, psum_t):
+                c, j = divmod(served[0], 4)
+                candidate_multiply(c, j, pool)
+                candidate_add(c, j)
+                added.append((c, j))
+                served[0] += 1
+            finish_tiles()
+            if served[0] == 26:
                 reset_quantise(last, 0, CHUNK)

@@ -19,8 +19,8 @@ K = 512
 CHUNK = 512
 N_CHUNKS = ROWS // CHUNK
 GAMMA = 0.01
-WOVEN = [0, 0, 0, 0, 0, 6, 6, 4]
-V_ROWS = [512, 512, 512, 384, 128, 128, 384, 0]
+WOVEN = [0, 0, 0, 0, 0, 4, 6, 2]
+V_ROWS = [512, 512, 512, 512, 256, 128, 384, 0]
 
 
 def tile_agrucell_pa_t_kernel(tc, x, h_prev, W_r, b_r, U_r, V_h, b_h, W_h, out):
@@ -369,35 +369,37 @@ def tile_agrucell_pa_t_kernel(tc, x, h_prev, W_r, b_r, U_r, V_h, b_h, W_h, out):
                 reset_product(c, first, P, False)
 
         for c in range(N_CHUNKS):
-            if ok(c - 1):
-                product_on_gpsimd(c - 1)
+            if ok(c + 1):
+                banks_x = input_transposes(c + 1, "x", None)
             if ok(c - 2) and V_ROWS[c - 2] < CHUNK:
                 reset_quantise(c - 2, 0, CHUNK)
             if ok(c + 1):
-                banks_x = input_transposes(c + 1, "x", None)
                 banks_h = input_transposes(c + 1, "h", None)
             multiply_tiles(WOVEN[c] // 2)
             if ok(c + 1):
-                input_leave(c + 1, "x", banks_x, "VS")
+                input_leave(c + 1, "x", banks_x, "VS" if c < 4 else "SS")
             add_tiles()
             if ok(c + 1):
                 input_leave(c + 1, "h", banks_h, "SS")
-            gate(c, 0)
             finish_tiles()
             multiply_tiles(WOVEN[c] // 2)
             add_tiles()
+            gate(c, 0)
             if ok(c - 1) and V_ROWS[c - 1] > 0:
                 reset_product(c - 1, 0, V_ROWS[c - 1], True)
             if ok(c + 1):
                 input_quantise(c + 1, "x")
-            for t in (1, 2, 3):
-                gate(c, t)
-            finish_tiles()
+            gate(c, 1)
             if ok(c + 1):
                 input_quantise(c + 1, "h")
+            gate(c, 2)
+            gate(c, 3)
             if ok(c - 1) and V_ROWS[c - 1] == CHUNK:
                 reset_quantise(c - 1, 0, CHUNK)
             weights_after_round(c)
+            if ok(c - 1):
+                product_on_gpsimd(c - 1)
+            finish_tiles()
 
         product_on_gpsimd(last)
         reset_quantise(last - 1, 0, CHUNK)

from contextlib import ExitStack

import concourse.mybir as mybir
from concourse.masks import make_identity

F32 = mybir.dt.float32
BF16 = mybir.dt.bfloat16
U32 = mybir.dt.uint32
U8 = mybir.dt.uint8
FP8X4 = mybir.dt.float8_e4m3fn_x4
ACT = mybir.ActivationFunctionType
ALU = mybir.AluOpType

FLOPS = 4 * 2 * 4096 * 512 * 512

P = 128
ROWS = 4096
K = 512
CHUNK = 512
N_CHUNKS = ROWS // CHUNK
GAMMA = 0.01
WOVEN = [0, 0, 0, 0, 0, 4, 6, 2]
V_ROWS = [512, 512, 512, 512, 256, 128, 384, 0]


def tile_agrucell_pa_t_kernel(tc, x, h_prev, W_r, b_r, U_r, V_h, b_h, W_h, out):
    nc = tc.nc
    with ExitStack() as ctx:
        ctx.enter_context(tc.manual_schedule())
        keep = ctx.enter_context(tc.tile_pool(name="keep", bufs=1))
        work = ctx.enter_context(tc.tile_pool(name="work", bufs=2))
        io = ctx.enter_context(tc.tile_pool(name="io", bufs=2 * N_CHUNKS))
        psum_t = ctx.enter_context(tc.psum_pool(name="psum_t", bufs=4))
        psum_g = ctx.enter_context(tc.psum_pool(name="psum_g", bufs=4))

        br_raw = keep.tile([P, 4], BF16, name="br_raw")
        with nc.allow_non_contiguous_dma(reason="512 bias values, two to a piece"):
            nc.scalar.dma_start(
                out=br_raw[:].rearrange("p (u e) -> p u e", u=2),
                in_=b_r.rearrange("(u p e) -> p u e", u=2, p=P, e=2),
            )
        bh_row = keep.tile([P, K], BF16, name="bh_row")
        nc.vector.memset(bh_row[:], 0.0)
        nc.scalar.dma_start(out=bh_row[0:1, :], in_=b_h.unsqueeze(0))

        warm = keep.tile([P, 1], F32, name="warm")
        nc.vector.memset(warm[:], 0.0)
        nc.scalar.activation(out=warm[:], in_=warm[:], func=ACT.Sigmoid)

        ident_f = keep.tile([P, P], F32, name="ident_f")
        make_identity(nc, ident_f[:])

        def load_weight(name, src, paired):
            raw = keep.tile([P, 4 * K], BF16, name=name)
            if paired:
                nc.sync.dma_start(
                    out=raw[:].rearrange("p (u f) -> p u f", u=2),
                    in_=src.rearrange("(u p e) k -> p u (e k)", u=2, p=P, e=2),
                )
            else:
                nc.sync.dma_start(
                    out=raw[:].rearrange("p (j k) -> p j k", j=4),
                    in_=src.rearrange("(j p) k -> p j k", p=P),
                )
            return raw

        x_rows = x.rearrange("(c p j) k -> c p (j k)", p=P, j=4)
        h_rows = h_prev.rearrange("(c p j) k -> c p (j k)", p=P, j=4)
        out_rows = out.rearrange("(c p j) n -> c p (j n)", p=P, j=4)
        x_raw = {}
        h_raw = {}

        def load_x(c):
            x_raw[c] = io.tile([P, 4 * K], BF16, name="x_raw%d" % c, tag="io")
            nc.sync.dma_start(out=x_raw[c][:], in_=x_rows[c])

        def load_h(c):
            h_raw[c] = io.tile([P, 4 * K], BF16, name="h_raw%d" % c, tag="io")
            nc.sync.dma_start(out=h_raw[c][:], in_=h_rows[c])

        wr_raw = load_weight("wr_raw", W_r, True)
        load_x(0)
        ur_raw = load_weight("ur_raw", U_r, True)
        load_h(0)
        for c in (1, 2):
            load_x(c)
            load_h(c)
        vh_raw = load_weight("vh_raw", V_h, False)
        wn_raw = load_weight("wn_raw", W_h, False)
        wk_raw = load_weight("wk_raw", W_h, True)
        for c in range(3, N_CHUNKS):
            load_x(c)
            load_h(c)

        ident_b = keep.tile([P, P], BF16, name="ident_b")
        nc.vector.tensor_copy(out=ident_b[:], in_=ident_f[:])
        neg_ident = keep.tile([P, P], BF16, name="neg_ident")
        nc.vector.tensor_scalar_mul(out=neg_ident[:], in0=ident_f[:], scalar1=-1.0)
        ones = keep.tile([P, P], BF16, name="ones")
        nc.vector.memset(ones[:], 1.0)
        damp = keep.tile([P, 2 * 256], BF16, name="damp")
        nc.vector.memset(damp[:], 0.0)
        damp_v = damp[:].rearrange("p (e q f) -> p e f q", e=2, q=P, f=2)
        for e in range(2):
            nc.vector.tensor_scalar_mul(out=damp_v[:, e, e, :], in0=ident_f[:], scalar1=-GAMMA)
        br = keep.tile([P, 4], F32, name="br")
        nc.vector.tensor_copy(out=br[:], in_=br_raw[:])

        def leave(engine, dst, src):
            if engine == "S":
                nc.scalar.copy(out=dst, in_=src)
            else:
                nc.vector.tensor_copy(out=dst, in_=src)

        def transpose_half(raw, half):
            words = raw[:].bitcast(F32)
            bank = psum_t.tile([P, 512], F32, name="bank_t", tag="t")
            for u in range(2):
                for jj in range(2):
                    j = 2 * half + jj
                    nc.tensor.transpose(
                        bank[:, (2 * u + jj) * P : (2 * u + jj + 1) * P],
                        words[:, 256 * j + P * u : 256 * j + P * u + P],
                        ident_f[:],
                    )
            return bank

        def leave_half(engine, bank, grouped, half):
            dst = grouped[:].bitcast(F32).rearrange("p (c u) -> p c u", u=2)
            leave(
                engine,
                dst[:, 256 * half : 256 * half + 256, :],
                bank[:].rearrange("p (u c) -> p c u", u=2),
            )

        def quantise(grouped, codes, scales, first, width):
            nc.vector.quantize_mx(
                out=codes[:, first : first + width].bitcast(FP8X4),
                scales=scales[:, first : first + width],
                in_=grouped[:, 4 * first : 4 * (first + width)],
            )

        weights = {}

        def weight_transposes(raw, engines):
            grouped = work.tile([P, 4 * K], BF16, name="w_g", tag="w_g", bufs=2, align_bytes=64)
            banks = [transpose_half(raw, 0), transpose_half(raw, 1)]
            for half in range(2):
                leave_half(engines[half], banks[half], grouped, half)
            return grouped

        def weight_quantise(name, grouped):
            codes = keep.tile([P, K], U32, name=name + "_c", align_bytes=64)
            scales = keep.tile([P, K], U8, name=name + "_s", align_bytes=64)
            quantise(grouped, codes, scales, 0, K)
            weights[name] = (codes, scales)

        last = N_CHUNKS - 1
        tiles = {}
        for c in range(N_CHUNKS):
            tiles[c] = {}

        def ok(c):
            return 0 <= c < N_CHUNKS

        def input_transposes(c, which, engines):
            d = tiles[c]
            raw = x_raw[c] if which == "x" else h_raw[c]
            grouped = work.tile(
                [P, 4 * CHUNK], BF16, name=which + "g", tag=which + "g", bufs=(2 if which == "x" else 3), align_bytes=64
            )
            d[which + "g"] = grouped
            return [transpose_half(raw, 0), transpose_half(raw, 1)]

        def input_leave(c, which, banks, engines):
            for half in range(2):
                leave_half(engines[half], banks[half], tiles[c][which + "g"], half)

        def input_quantise(c, which):
            d = tiles[c]
            if which == "x":
                codes = keep.tile([P, CHUNK], U32, name="xc%d" % c, align_bytes=64)
                scales = keep.tile([P, CHUNK], U8, name="xs%d" % c, align_bytes=64)
            else:
                codes = work.tile([P, CHUNK], U32, name="hc", tag="hc", bufs=2, align_bytes=64)
                scales = work.tile([P, CHUNK], U8, name="hs", tag="hs", bufs=2, align_bytes=64)
            quantise(d[which + "g"], codes, scales, 0, CHUNK)
            d[which] = (codes, scales)

        def mx(acc, a, a_cols, b, b_cols, start, stop):
            nc.tensor.matmul_mx(
                out=acc,
                lhsT=a[0][:, a_cols].bitcast(FP8X4),
                lhsT_scale=a[1][:, a_cols],
                rhs=b[0][:, b_cols].bitcast(FP8X4),
                rhs_scale=b[1][:, b_cols],
                start=start,
                stop=stop,
            )

        everything = slice(0, 512)

        def gate(c, t):
            d = tiles[c]
            if t == 0:
                d["r"] = work.tile([P, 4 * CHUNK], F32, name="r", tag="r", bufs=3)
            cols = slice(P * t, P * t + P)
            acc = psum_g.tile([P, CHUNK], F32, name="acc1", tag="g")
            mx(acc[:], weights["wr"], cols, d["x"], everything, True, False)
            mx(acc[:], weights["ur"], cols, d["h"], everything, False, True)
            nc.scalar.activation(
                out=d["r"][:, CHUNK * t : CHUNK * (t + 1)],
                in_=acc[:],
                func=ACT.Sigmoid,
                bias=br[:, t : t + 1],
                scale=1.0,
            )

        def reset_product(c, first, width, on_vector):
            d = tiles[c]
            if "hrg" not in d:
                d["hrg"] = work.tile([P, 4 * CHUNK], BF16, name="hrg", tag="hrg", bufs=3, align_bytes=64)
            if on_vector:
                runs = slice(first // 2, (first + width) // 2)
                nc.vector.tensor_tensor(
                    out=d["hrg"][:].rearrange("p (c i t) -> p c t i", i=2, t=4)[:, runs, :, :],
                    in0=d["r"][:].rearrange("p (t c i) -> p c t i", t=4, i=2)[:, runs, :, :],
                    in1=d["hg"][:].rearrange("p (c i t) -> p c t i", i=2, t=4)[:, runs, :, :],
                    op=ALU.mult,
                )
            else:
                rows = slice(first, first + width)
                nc.gpsimd.tensor_tensor(
                    out=d["hrg"][:].rearrange("p (b t) -> p b t", t=4)[:, rows, :],
                    in0=d["r"][:].rearrange("p (t b) -> p b t", t=4)[:, rows, :],
                    in1=d["hg"][:].rearrange("p (b t) -> p b t", t=4)[:, rows, :],
                    op=ALU.mult,
                )

        def reset_quantise(c, first, width):
            d = tiles[c]
            if "hr" not in d:
                codes = keep.tile([P, CHUNK], U32, name="hrc%d" % c, align_bytes=64)
                scales = keep.tile([P, CHUNK], U8, name="hrs%d" % c, align_bytes=64)
                d["hr"] = (codes, scales)
            quantise(d["hrg"], d["hr"][0], d["hr"][1], first, width)

        def candidate_multiply(c, j, pool):
            d = tiles[c]
            cols = slice(P * j, P * j + P)
            if pool is psum_t:
                acc = psum_t.tile([P, K], F32, name="acc2t", tag="t")
            else:
                acc = psum_g.tile([P, K], F32, name="acc2g", tag="g")
            mx(acc[:], d["x"], cols, weights["vh"], everything, True, False)
            mx(acc[:], d["hr"], cols, weights["a"], everything, False, True)
            d["acc%d" % j] = acc

        def candidate_add(c, j):
            d = tiles[c]
            if j % 2 == 0:
                d["z%d" % (j // 2)] = io.tile([P, 2 * K], F32, name="z", tag="io")
            nc.vector.tensor_tensor(
                out=d["z%d" % (j // 2)][:, K * (j % 2) : K * (j % 2 + 1)],
                in0=d["acc%d" % j][:],
                in1=bias_bc[:],
                op=ALU.add,
            )

        def finish(c, j0, j1):
            z = tiles[c]["z%d" % (j0 // 2)]
            span = slice(K * (j0 % 2), K * (j0 % 2) + K * (j1 - j0))
            nc.scalar.activation(out=z[:, span], in_=z[:, span], func=ACT.Tanh)
            nc.sync.dma_start(out=out_rows[c][:, K * j0 : K * j1], in_=z[:, span])

        bias_bc = keep.tile([P, K], F32, name="bias_bc")

        vh_g = work.tile([P, 4 * K], BF16, name="vh_g", tag="vh_g", bufs=1, align_bytes=64)
        a_g = work.tile([P, 4 * K], BF16, name="a_g", tag="a_g", bufs=1, align_bytes=64)

        def vh_half(half, engine):
            leave_half(engine, transpose_half(vh_raw, half), vh_g, half)

        def a_block(j, engine):
            a_gv = a_g[:].rearrange("p (c t) -> p c t", t=4)
            wn_v = wn_raw[:].rearrange("p (j u q e) -> p j u e q", j=4, u=2, q=P, e=2)
            bank = psum_t.tile([P, 512], F32, name="bank_a", tag="t")
            for t in range(4):
                u, e = divmod(t, 2)
                region = bank[:, P * t : P * t + P]
                on_diagonal = j // 2 == u
                nc.tensor.matmul(
                    region,
                    lhsT=neg_ident[:],
                    rhs=wk_raw[:, K * t + P * j : K * t + P * j + P],
                    start=True,
                    stop=False,
                )
                nc.tensor.matmul(region, lhsT=wn_v[:, j, u, e, :], rhs=ident_b[:], start=False, stop=not on_diagonal)
                if on_diagonal:
                    nc.tensor.matmul(
                        region,
                        lhsT=ident_b[:],
                        rhs=damp[:, 256 * e + P * (j % 2) : 256 * e + P * (j % 2) + P],
                        start=False,
                        stop=True,
                    )
            leave(engine, a_gv[:, P * j : P * j + P, :], bank[:].rearrange("p (t q) -> p q t", t=4))

        def bias_block():
            bank_b = psum_t.tile([P, 512], F32, name="bank_b", tag="t")
            nc.tensor.matmul(bank_b[:], lhsT=ones[:], rhs=bh_row[:], start=True, stop=True)
            nc.vector.tensor_copy(out=bias_bc[:], in_=bank_b[:])

        def weights_after_round(c):
            if c == 1:
                vh_half(1, "S")
                vh_half(0, "V")
                weight_quantise("vh", vh_g)
                a_block(0, "S")
            elif c == 2:
                a_block(1, "S")
            elif c == 3:
                a_block(2, "S")
                a_block(3, "S")
                bias_block()
            elif c == 4:
                weight_quantise("a", a_g)

        wr_g = weight_transposes(wr_raw, ("V", "S"))
        banks = input_transposes(0, "x", None)
        input_leave(0, "x", banks, ("V", "S"))
        weight_quantise("wr", wr_g)
        ur_g = weight_transposes(ur_raw, ("V", "S"))
        input_quantise(0, "x")
        banks = input_transposes(0, "h", None)
        input_leave(0, "h", banks, ("V", "S"))
        weight_quantise("ur", ur_g)
        input_quantise(0, "h")

        served = [0]
        summed = []
        added = []

        def multiply_tiles(count):
            for i in range(count):
                c, j = divmod(served[0], 4)
                candidate_multiply(c, j, psum_g)
                summed.append((c, j))
                served[0] += 1

        def add_tiles():
            for c, j in summed:
                candidate_add(c, j)
            added.extend(summed)
            summed.clear()

        def finish_tiles():
            while added and (len(added) > 1 or added[0] >= (last, 2)):
                c, j = added.pop(0)
                if (c, j) >= (last, 2):
                    finish(c, j, j + 1)
                else:
                    added.pop(0)
                    finish(c, j, j + 2)

        def product_on_gpsimd(c):
            for first in range(V_ROWS[c], CHUNK, P):
                reset_product(c, first, P, False)

        for c in range(N_CHUNKS):
            if ok(c + 1):
                banks_x = input_transposes(c + 1, "x", None)
            if ok(c - 2) and V_ROWS[c - 2] < CHUNK:
                reset_quantise(c - 2, 0, CHUNK)
            if ok(c + 1):
                banks_h = input_transposes(c + 1, "h", None)
            multiply_tiles(WOVEN[c] // 2)
            if ok(c + 1):
                input_leave(c + 1, "x", banks_x, "VS" if c < 4 else "SS")
            add_tiles()
            if ok(c + 1):
                input_leave(c + 1, "h", banks_h, "SS")
            finish_tiles()
            multiply_tiles(WOVEN[c] // 2)
            add_tiles()
            gate(c, 0)
            if ok(c - 1) and V_ROWS[c - 1] > 0:
                reset_product(c - 1, 0, V_ROWS[c - 1], True)
            if ok(c + 1):
                input_quantise(c + 1, "x")
            gate(c, 1)
            if ok(c + 1):
                input_quantise(c + 1, "h")
            gate(c, 2)
            gate(c, 3)
            if ok(c - 1) and V_ROWS[c - 1] == CHUNK:
                reset_quantise(c - 1, 0, CHUNK)
            weights_after_round(c)
            if ok(c - 1):
                product_on_gpsimd(c - 1)
            finish_tiles()

        product_on_gpsimd(last)
        reset_quantise(last - 1, 0, CHUNK)
        while served[0] < 4 * N_CHUNKS:
            for pool in (psum_g, psum_t):
                c, j = divmod(served[0], 4)
                candidate_multiply(c, j, pool)
                candidate_add(c, j)
                added.append((c, j))
                served[0] += 1
            finish_tiles()
            if served[0] == 26:
                reset_quantise(last, 0, CHUNK)
